import numpy as np
import ml_dtypes


def mxq(x, axis, fmt="e4m3"):
    dtype, down = {"e4m3": (ml_dtypes.float8_e4m3fn, 7), "e5m2": (ml_dtypes.float8_e5m2, 14)}[fmt]
    v = np.moveaxis(np.asarray(x, np.float32).astype(ml_dtypes.bfloat16).astype(np.float64), axis, -1)
    blocks = v.reshape(v.shape[:-1] + (-1, 32))
    amax = np.abs(blocks).max(-1, keepdims=True)
    byte = np.maximum(np.where(amax > 0, np.frexp(amax)[1] - 1 + 127, 0) - down, 1)
    scale = np.exp2(byte - 127.0)
    codes = (blocks / scale).astype(np.float32).astype(dtype).astype(np.float64)
    return np.moveaxis((codes * scale).reshape(v.shape), -1, axis)


WIDE = False


def mx_kscale(k):
    if not WIDE:
        return np.ones(k)
    levels = np.array([10, -10, 5, -5, 0])
    a = np.random.permutation(np.resize(levels, k // 512 * 4)).reshape(k // 512, 4)
    idx = np.arange(k)
    return np.exp2(a[idx // 512, idx % 128 // 32])


BF16 = ml_dtypes.bfloat16


def bf(x):
    return np.asarray(x, np.float32).astype(BF16)


def f64(x):
    return np.asarray(x).astype(np.float64)


G, GI, GO, B = 32, 32, 32, 4096
K = G * GI
N = G * GO


def block_gain():
    gain = np.ones((N, K))
    for g in range(G):
        gain[g * GO:(g + 1) * GO, g * GI:(g + 1) * GI] = 0.5
    return gain


def setup_inputs():
    s = mx_kscale(K)
    bound = 1.0 / np.sqrt(K)
    W = np.random.uniform(-bound, bound, (N, K)) * block_gain()
    return {"data": bf(np.random.standard_normal((B, K)) * s),
            "W": bf(W / s[None, :]),
            "b": bf(np.random.standard_normal(N) * 0.3)}


def reference(data, W, b):
    return (mxq(f64(data), 1, "e4m3") @ mxq(f64(W), 1, "e4m3").T) + f64(b)

@@ -1,0 +1,182 @@
+from contextlib import ExitStack
+
+import concourse.mybir as mybir
+from concourse.masks import make_identity
+
+F32 = mybir.dt.float32
+BF16 = mybir.dt.bfloat16
+U32 = mybir.dt.uint32
+U8 = mybir.dt.uint8
+FP8X4 = mybir.dt.float8_e4m3fn_x4
+ADD = mybir.AluOpType.add
+
+P = 128
+B = 4096
+K = 1024
+N = 1024
+FLOPS = 2 * B * K * N
+NT = B // P
+NW = N // P
+KW = K // 2
+NB = 512
+
+GROUPS = [2] * 16
+CHUNKS = [2, 2, 4, 4, 4, 4, 4, 4, 4]
+S = 2
+
+
+def tile_groupfc_kernel(tc, data, W, b, out):
+    nc = tc.nc
+    assert sum(GROUPS) == NT and sum(CHUNKS) == NT
+    with ExitStack() as ctx:
+        const = ctx.enter_context(tc.tile_pool(name="const", bufs=1))
+        grp = ctx.enter_context(tc.tile_pool(name="grp", bufs=3))
+        stage = ctx.enter_context(tc.tile_pool(name="stage", bufs=8))
+        psum = ctx.enter_context(tc.psum_pool(name="psum", bufs=8))
+        ctx.enter_context(tc.manual_schedule())
+
+        data_v = data.rearrange("(p t) k -> p (t k)", t=NT)
+        out_v = out.rearrange("(p t) n -> p (t n)", t=NT)
+        w_v = W.rearrange("(t p) k -> t p k", p=P)
+
+        ident = const.tile([P, P], F32, name="ident")
+        make_identity(nc, ident[:])
+        ones = const.tile([P, P], BF16, name="ones")
+        nc.vector.memset(ones[:], 1.0)
+        brow = const.tile([P, N], BF16, name="brow")
+        nc.vector.memset(brow[:], 0.0)
+        nc.scalar.dma_start(out=brow[0:1, :], in_=b.unsqueeze(0))
+        bias = const.tile([P, N], F32, name="bias")
+
+        w_sb = []
+        x_sb = []
+        where = []
+        for c in range(len(CHUNKS)):
+            for l in range(CHUNKS[c]):
+                where.append((c, l))
+
+        def load_w(t):
+            wt = const.tile([P, K], BF16, name="w%d" % t)
+            nc.sync.dma_start(out=wt[:], in_=w_v[t])
+            w_sb.append(wt)
+
+        def load_x(c):
+            t0 = sum(CHUNKS[:c])
+            xt = const.tile([P, CHUNKS[c] * K], BF16, name="x%d" % c)
+            nc.sync.dma_start(out=xt[:], in_=data_v[:, t0 * K:(t0 + CHUNKS[c]) * K])
+            x_sb.append(xt)
+
+        for t in range(4):
+            load_w(t)
+        load_x(0)
+        for t in range(4, 8):
+            load_w(t)
+        for c in range(1, len(CHUNKS)):
+            load_x(c)
+
+        gw = const.tile([P, 4 * N * 2], BF16, name="gw", align_bytes=64)
+        gw_f = gw[:].bitcast(F32).rearrange("p (g n u) -> p g n u", g=2, u=2)
+        wq = const.tile([P, 2 * N], U32, name="wq", align_bytes=64)
+        ws = const.tile([P, 2 * N], U8, name="ws", align_bytes=64)
+
+        def transposes(src_f32, off):
+            pt = psum.tile([P, NB], F32, name="pt", tag="ps")
+            for c in range(4):
+                nc.tensor.transpose(pt[:, c * P:(c + 1) * P], src_f32[:, off + c * P: off + (c + 1) * P], ident[:])
+            return pt[:].rearrange("p (g u r) -> p g r u", g=2, u=2)
+
+        def tw(t, eng):
+            src = transposes(w_sb[t][:].bitcast(F32), 0)
+            dst = gw_f[:, :, t * P:(t + 1) * P, :]
+            if eng == 0:
+                nc.scalar.copy(out=dst, in_=src)
+            else:
+                nc.vector.tensor_copy(out=dst, in_=src)
+
+        def qw(t):
+            for g in range(2):
+                c0 = g * N + t * P
+                nc.vector.quantize_mx(
+                    out=wq[:, c0:c0 + P].bitcast(FP8X4),
+                    scales=ws[:, c0:c0 + P],
+                    in_=gw[:, 4 * c0:4 * (c0 + P)],
+                )
+
+        xg = {}
+        xq = {}
+        xs = {}
+        first = [sum(GROUPS[:j]) for j in range(len(GROUPS))]
+
+        def tr(j):
+            r = GROUPS[j]
+            xg[j] = grp.tile([P, r * K], BF16, name="xg", tag="xg", align_bytes=64)
+            xg_f = xg[j][:].bitcast(F32)
+            for l in range(r):
+                c, i = where[first[j] + l]
+                src = transposes(x_sb[c][:].bitcast(F32), i * KW)
+                dst = xg_f[:, l * KW:(l + 1) * KW].rearrange("p (g r u) -> p g r u", g=2, u=2)
+                nc.scalar.copy(out=dst, in_=src)
+
+        def qx(j):
+            r = GROUPS[j]
+            xq[j] = grp.tile([P, r * 256], U32, name="xq", tag="xq", align_bytes=64)
+            xs[j] = grp.tile([P, r * 256], U8, name="xs", tag="xs", align_bytes=64)
+            nc.vector.quantize_mx(out=xq[j][:].bitcast(FP8X4), scales=xs[j][:], in_=xg[j][:])
+
+        cur = {}
+
+        def mm(j):
+            for l in range(GROUPS[j]):
+                t = first[j] + l
+                if t % S == 0:
+                    cur["ot"] = stage.tile([P, S * N], F32, name="ot", tag="ot")
+                ot = cur["ot"]
+                for h in range(2):
+                    acc = psum.tile([P, NB], F32, name="acc", tag="ps")
+                    for g in range(2):
+                        a0 = l * 256 + g * P
+                        b0 = g * N + h * NB
+                        nc.tensor.matmul_mx(
+                            out=acc[:],
+                            lhsT=xq[j][:, a0:a0 + P].bitcast(FP8X4),
+                            lhsT_scale=xs[j][:, a0:a0 + P],
+                            rhs=wq[:, b0:b0 + NB].bitcast(FP8X4),
+                            rhs_scale=ws[:, b0:b0 + NB],
+                            start=(g == 0),
+                            stop=(g == 1),
+                        )
+                    o0 = (t % S) * N + h * NB
+                    nc.vector.tensor_tensor(out=ot[:, o0:o0 + NB], in0=acc[:], in1=bias[:, h * NB:(h + 1) * NB], op=ADD)
+                if t % S == S - 1:
+                    nc.sync.dma_start(out=out_v[:, (t - S + 1) * N:(t + 1) * N], in_=ot[:])
+
+        tw(0, 0)
+        tw(1, 1)
+        qw(0)
+        tw(2, 0)
+        tw(3, 1)
+        qw(1)
+        qw(2)
+        for h in range(2):
+            pb = psum.tile([P, NB], F32, name="pb", tag="ps")
+            nc.tensor.matmul(out=pb[:], lhsT=ones[:], rhs=brow[:, h * NB:(h + 1) * NB], start=True, stop=True)
+            nc.scalar.copy(out=bias[:, h * NB:(h + 1) * NB], in_=pb[:])
+        tr(0)
+        qw(3)
+        tw(4, 0)
+        tw(5, 1)
+        qw(4)
+        tw(6, 0)
+        tw(7, 1)
+        qw(5)
+        qw(6)
+        tr(1)
+        qw(7)
+        qx(0)
+        ng = len(GROUPS)
+        for j in range(ng):
+            if j + 2 < ng:
+                tr(j + 2)
+            if j + 1 < ng:
+                qx(j + 1)
+            mm(j)

@@ -16,22 +16,30 @@ K = 1024
 N = 1024
 FLOPS = 2 * B * K * N
 NT = B // P
-NW = N // P
 KW = K // 2
 NB = 512
+QT = 256
+ST = 4
 
-GROUPS = [2] * 16
-CHUNKS = [2, 2, 4, 4, 4, 4, 4, 4, 4]
-S = 2
+GROUPS = [1,1,2,4,4,4,4,4,4,4]
+LOADS = [("x", 0, 1), ("w", 0, 1), ("w", 1, 1), ("w", 2, 1), ("w", 3, 1), ("x", 1, 1), ("x", 2, 2),
+         ("w", 4, 1), ("w", 5, 1), ("w", 6, 1), ("w", 7, 1), ("x", 4, 4), ("x", 8, 8), ("x", 16, 16)]
+UNITS = [8,8,8,4,4,4,4,4,4,2,2,2,2,2,2,2,1,1]
+QPOS = 2
+VIA_MOD = 0
+VIA_TAIL_FROM = 0
+VIA_TAIL_MOD = 0
+WARM = 0
+WARM_EACH = 0
 
 
 def tile_groupfc_kernel(tc, data, W, b, out):
     nc = tc.nc
-    assert sum(GROUPS) == NT and sum(CHUNKS) == NT
+    assert sum(GROUPS) == NT and sum(UNITS) == 2 * NT
     with ExitStack() as ctx:
         const = ctx.enter_context(tc.tile_pool(name="const", bufs=1))
-        grp = ctx.enter_context(tc.tile_pool(name="grp", bufs=3))
-        stage = ctx.enter_context(tc.tile_pool(name="stage", bufs=8))
+        grp = ctx.enter_context(tc.tile_pool(name="grp", bufs=2))
+        stage = ctx.enter_context(tc.tile_pool(name="stage", bufs=4))
         psum = ctx.enter_context(tc.psum_pool(name="psum", bufs=8))
         ctx.enter_context(tc.manual_schedule())
 
@@ -39,45 +47,46 @@ def tile_groupfc_kernel(tc, data, W, b, out):
         out_v = out.rearrange("(p t) n -> p (t n)", t=NT)
         w_v = W.rearrange("(t p) k -> t p k", p=P)
 
-        ident = const.tile([P, P], F32, name="ident")
-        make_identity(nc, ident[:])
         ones = const.tile([P, P], BF16, name="ones")
         nc.vector.memset(ones[:], 1.0)
         brow = const.tile([P, N], BF16, name="brow")
         nc.vector.memset(brow[:], 0.0)
         nc.scalar.dma_start(out=brow[0:1, :], in_=b.unsqueeze(0))
+        scr = const.tile([P, 8], F32, name="scr")
+        nc.scalar.copy(out=scr[:, 0:1], in_=ones[:, 0:1])
+        ident = const.tile([P, P], F32, name="ident")
+        make_identity(nc, ident[:])
         bias = const.tile([P, N], F32, name="bias")
 
-        w_sb = []
-        x_sb = []
-        where = []
-        for c in range(len(CHUNKS)):
-            for l in range(CHUNKS[c]):
-                where.append((c, l))
+        w_sb = {}
+        x_at = {}
+        for kind, t0, n in LOADS:
+            if kind == "w":
+                wt = const.tile([P, K], BF16, name="w%d" % t0)
+                nc.sync.dma_start(out=wt[:], in_=w_v[t0])
+                w_sb[t0] = wt
+            else:
+                xt = const.tile([P, n * K], BF16, name="x%d" % t0)
+                nc.sync.dma_start(out=xt[:], in_=data_v[:, t0 * K:(t0 + n) * K])
+                for i in range(n):
+                    x_at[t0 + i] = (xt[:].bitcast(F32), i * KW)
 
-        def load_w(t):
-            wt = const.tile([P, K], BF16, name="w%d" % t)
-            nc.sync.dma_start(out=wt[:], in_=w_v[t])
-            w_sb.append(wt)
+        gw = []
+        gw_f = []
+        wq = []
+        ws = []
+        for h in range(2):
+            gwh = const.tile([P, 2 * NB * 4], BF16, name="gw%d" % h, align_bytes=64)
+            gw.append(gwh)
+            gw_f.append(gwh[:].bitcast(F32).rearrange("p (g n u) -> p g n u", g=2, u=2))
+            wq.append(const.tile([P, 2 * NB], U32, name="wq%d" % h, align_bytes=64))
+            ws.append(const.tile([P, 2 * NB], U8, name="ws%d" % h, align_bytes=64))
 
-        def load_x(c):
-            t0 = sum(CHUNKS[:c])
-            xt = const.tile([P, CHUNKS[c] * K], BF16, name="x%d" % c)
-            nc.sync.dma_start(out=xt[:], in_=data_v[:, t0 * K:(t0 + CHUNKS[c]) * K])
-            x_sb.append(xt)
-
-        for t in range(4):
-            load_w(t)
-        load_x(0)
-        for t in range(4, 8):
-            load_w(t)
-        for c in range(1, len(CHUNKS)):
-            load_x(c)
-
-        gw = const.tile([P, 4 * N * 2], BF16, name="gw", align_bytes=64)
-        gw_f = gw[:].bitcast(F32).rearrange("p (g n u) -> p g n u", g=2, u=2)
-        wq = const.tile([P, 2 * N], U32, name="wq", align_bytes=64)
-        ws = const.tile([P, 2 * N], U8, name="ws", align_bytes=64)
+        def dummies(n):
+            if n > 0:
+                dm = psum.tile([P, NB], F32, name="dm", tag="ps")
+                for i in range(n):
+                    nc.tensor.matmul(out=dm[:], lhsT=ones[:], rhs=brow[:, 0:NB], start=True, stop=True)
 
         def transposes(src_f32, off):
             pt = psum.tile([P, NB], F32, name="pt", tag="ps")
@@ -86,97 +95,167 @@ def tile_groupfc_kernel(tc, data, W, b, out):
             return pt[:].rearrange("p (g u r) -> p g r u", g=2, u=2)
 
         def tw(t, eng):
-            src = transposes(w_sb[t][:].bitcast(F32), 0)
-            dst = gw_f[:, :, t * P:(t + 1) * P, :]
-            if eng == 0:
-                nc.scalar.copy(out=dst, in_=src)
+            h = t // 4
+            n0 = (t % 4) * P
+            src_f32 = w_sb[t][:].bitcast(F32)
+            if eng == 2:
+                for g in range(2):
+                    ph = psum.tile([P, NB], F32, name="ph", tag="ps")
+                    for u in range(2):
+                        c = 2 * g + u
+                        nc.tensor.transpose(ph[:, u * P:(u + 1) * P], src_f32[:, c * P:(c + 1) * P], ident[:])
+                    src = ph[:, 0:2 * P].rearrange("p (u r) -> p r u", u=2)
+                    dst = gw_f[h][:, g, n0:n0 + P, :]
+                    if g == 0:
+                        nc.vector.tensor_copy(out=dst, in_=src)
+                    else:
+                        nc.scalar.copy(out=dst, in_=src)
             else:
-                nc.vector.tensor_copy(out=dst, in_=src)
+                src = transposes(src_f32, 0)
+                dst = gw_f[h][:, :, n0:n0 + P, :]
+                if eng == 0:
+                    nc.scalar.copy(out=dst, in_=src)
+                else:
+                    nc.vector.tensor_copy(out=dst, in_=src)
+            dummies(WARM_EACH)
 
         def qw(t):
+            h = t // 4
             for g in range(2):
-                c0 = g * N + t * P
+                c0 = g * NB + (t % 4) * P
                 nc.vector.quantize_mx(
-                    out=wq[:, c0:c0 + P].bitcast(FP8X4),
-                    scales=ws[:, c0:c0 + P],
-                    in_=gw[:, 4 * c0:4 * (c0 + P)],
+                    out=wq[h][:, c0:c0 + P].bitcast(FP8X4),
+                    scales=ws[h][:, c0:c0 + P],
+                    in_=gw[h][:, 4 * c0:4 * (c0 + P)],
                 )
 
         xg = {}
         xq = {}
         xs = {}
         first = [sum(GROUPS[:j]) for j in range(len(GROUPS))]
+        HEAD = 3
 
         def tr(j):
             r = GROUPS[j]
-            xg[j] = grp.tile([P, r * K], BF16, name="xg", tag="xg", align_bytes=64)
+            if j < HEAD:
+                xg[j] = const.tile([P, r * K], BF16, name="xgh%d" % j, align_bytes=64)
+            else:
+                xg[j] = grp.tile([P, r * K], BF16, name="xg", tag="xg", align_bytes=64)
             xg_f = xg[j][:].bitcast(F32)
             for l in range(r):
-                c, i = where[first[j] + l]
-                src = transposes(x_sb[c][:].bitcast(F32), i * KW)
+                src_f32, off = x_at[first[j] + l]
+                src = transposes(src_f32, off)
                 dst = xg_f[:, l * KW:(l + 1) * KW].rearrange("p (g r u) -> p g r u", g=2, u=2)
                 nc.scalar.copy(out=dst, in_=src)
 
         def qx(j):
             r = GROUPS[j]
-            xq[j] = grp.tile([P, r * 256], U32, name="xq", tag="xq", align_bytes=64)
-            xs[j] = grp.tile([P, r * 256], U8, name="xs", tag="xs", align_bytes=64)
+            if j < HEAD:
+                xq[j] = const.tile([P, r * QT], U32, name="xqh%d" % j, align_bytes=64)
+                xs[j] = const.tile([P, r * QT], U8, name="xsh%d" % j, align_bytes=64)
+            else:
+                xq[j] = grp.tile([P, r * QT], U32, name="xq", tag="xq", align_bytes=64)
+                xs[j] = grp.tile([P, r * QT], U8, name="xs", tag="xs", align_bytes=64)
             nc.vector.quantize_mx(out=xq[j][:].bitcast(FP8X4), scales=xs[j][:], in_=xg[j][:])
 
-        cur = {}
+        unit_of = []
+        unit_b0 = []
+        left = []
+        for i in range(len(UNITS)):
+            unit_b0.append(len(unit_of))
+            left.append(UNITS[i])
+            for k in range(UNITS[i]):
+                unit_of.append(i)
+        staging = {}
 
-        def mm(j):
+        def via(bk):
+            if VIA_TAIL_MOD > 0 and bk >= VIA_TAIL_FROM:
+                return bk % VIA_TAIL_MOD == 1
+            return VIA_MOD > 0 and bk % VIA_MOD == 1
+
+        def bank(j, l, h):
+            t = first[j] + l
+            bk = 2 * t + h
+            s = t // ST
+            if s not in staging:
+                staging[s] = stage.tile([P, ST * N], F32, name="ot", tag="ot")
+            ot = staging[s]
+            acc = psum.tile([P, NB], F32, name="acc", tag="ps")
+            for g in range(2):
+                a0 = l * QT + g * P
+                nc.tensor.matmul_mx(
+                    out=acc[:],
+                    lhsT=xq[j][:, a0:a0 + P].bitcast(FP8X4),
+                    lhsT_scale=xs[j][:, a0:a0 + P],
+                    rhs=wq[h][:, g * NB:(g + 1) * NB].bitcast(FP8X4),
+                    rhs_scale=ws[h][:, g * NB:(g + 1) * NB],
+                    start=(g == 0),
+                    stop=(g == 1),
+                )
+            o0 = (bk % (2 * ST)) * NB
+            bs = bias[:, h * NB:(h + 1) * NB]
+            if via(bk):
+                nc.scalar.copy(out=ot[:, o0:o0 + NB], in_=acc[:])
+                nc.gpsimd.tensor_tensor(out=ot[:, o0:o0 + NB], in0=ot[:, o0:o0 + NB], in1=bs, op=ADD)
+            else:
+                nc.vector.tensor_tensor(out=ot[:, o0:o0 + NB], in0=acc[:], in1=bs, op=ADD)
+            i = unit_of[bk]
+            left[i] -= 1
+            if left[i] == 0:
+                b0 = unit_b0[i]
+                c0 = (b0 % (2 * ST)) * NB
+                w = UNITS[i] * NB
+                nc.sync.dma_start(out=out_v[:, b0 * NB:b0 * NB + w], in_=ot[:, c0:c0 + w])
+
+        def mm(j, hs, nxt):
+            k = 0
+            kq = min(QPOS, len(hs) * GROUPS[j])
             for l in range(GROUPS[j]):
-                t = first[j] + l
-                if t % S == 0:
-                    cur["ot"] = stage.tile([P, S * N], F32, name="ot", tag="ot")
-                ot = cur["ot"]
-                for h in range(2):
-                    acc = psum.tile([P, NB], F32, name="acc", tag="ps")
-                    for g in range(2):
-                        a0 = l * 256 + g * P
-                        b0 = g * N + h * NB
-                        nc.tensor.matmul_mx(
-                            out=acc[:],
-                            lhsT=xq[j][:, a0:a0 + P].bitcast(FP8X4),
-                            lhsT_scale=xs[j][:, a0:a0 + P],
-                            rhs=wq[:, b0:b0 + NB].bitcast(FP8X4),
-                            rhs_scale=ws[:, b0:b0 + NB],
-                            start=(g == 0),
-                            stop=(g == 1),
-                        )
-                    o0 = (t % S) * N + h * NB
-                    nc.vector.tensor_tensor(out=ot[:, o0:o0 + NB], in0=acc[:], in1=bias[:, h * NB:(h + 1) * NB], op=ADD)
-                if t % S == S - 1:
-                    nc.sync.dma_start(out=out_v[:, (t - S + 1) * N:(t + 1) * N], in_=ot[:])
+                for h in hs:
+                    bank(j, l, h)
+                    k += 1
+                    if nxt is not None and k == kq:
+                        qx(nxt)
 
-        tw(0, 0)
-        tw(1, 1)
-        qw(0)
-        tw(2, 0)
-        tw(3, 1)
-        qw(1)
-        qw(2)
+        dummies(WARM)
         for h in range(2):
             pb = psum.tile([P, NB], F32, name="pb", tag="ps")
             nc.tensor.matmul(out=pb[:], lhsT=ones[:], rhs=brow[:, h * NB:(h + 1) * NB], start=True, stop=True)
             nc.scalar.copy(out=bias[:, h * NB:(h + 1) * NB], in_=pb[:])
         tr(0)
+        tw(0, 0)
+        tw(1, 1)
+        qx(0)
+        qw(0)
+        tw(2, 0)
+        qw(1)
+        tw(3, 2)
+        qw(2)
         qw(3)
+        tr(1)
+        tr(2)
+        qx(1)
+        qx(2)
+        mm(0, [0], None)
+        mm(1, [0], None)
+        mm(2, [0], None)
         tw(4, 0)
         tw(5, 1)
         qw(4)
         tw(6, 0)
-        tw(7, 1)
         qw(5)
+        tw(7, 2)
         qw(6)
-        tr(1)
         qw(7)
-        qx(0)
+        tr(3)
+        mm(0, [1], None)
+        mm(1, [1], None)
+        qx(3)
+        mm(2, [1], None)
         ng = len(GROUPS)
-        for j in range(ng):
-            if j + 2 < ng:
-                tr(j + 2)
+        for j in range(HEAD, ng):
             if j + 1 < ng:
-                qx(j + 1)
-            mm(j)
+                tr(j + 1)
+                mm(j, [0, 1], j + 1)
+            else:
+                mm(j, [0, 1], None)

@@ -218,10 +218,6 @@ def tile_groupfc_kernel(tc, data, W, b, out):
                         qx(nxt)
 
         dummies(WARM)
-        for h in range(2):
-            pb = psum.tile([P, NB], F32, name="pb", tag="ps")
-            nc.tensor.matmul(out=pb[:], lhsT=ones[:], rhs=brow[:, h * NB:(h + 1) * NB], start=True, stop=True)
-            nc.scalar.copy(out=bias[:, h * NB:(h + 1) * NB], in_=pb[:])
         tr(0)
         tw(0, 0)
         tw(1, 1)
@@ -234,6 +230,10 @@ def tile_groupfc_kernel(tc, data, W, b, out):
         qw(3)
         tr(1)
         tr(2)
+        for h in range(2):
+            pb = psum.tile([P, NB], F32, name="pb", tag="ps")
+            nc.tensor.matmul(out=pb[:], lhsT=ones[:], rhs=brow[:, h * NB:(h + 1) * NB], start=True, stop=True)
+            nc.scalar.copy(out=bias[:, h * NB:(h + 1) * NB], in_=pb[:])
         qx(1)
         qx(2)
         mm(0, [0], None)

@@ -26,7 +26,7 @@ LOADS = [("x", 0, 1), ("w", 0, 1), ("w", 1, 1), ("w", 2, 1), ("w", 3, 1), ("x", 
          ("w", 4, 1), ("w", 5, 1), ("w", 6, 1), ("w", 7, 1), ("x", 4, 4), ("x", 8, 8), ("x", 16, 16)]
 UNITS = [8,8,8,4,4,4,4,4,4,2,2,2,2,2,2,2,1,1]
 QPOS = 2
-VIA_MOD = 0
+VIA_MOD = 4
 VIA_TAIL_FROM = 0
 VIA_TAIL_MOD = 0
 WARM = 0

@@ -20,15 +20,12 @@ KW = K // 2
 NB = 512
 QT = 256
 ST = 4
+BANKS = 8
 
-GROUPS = [1,1,2,4,4,4,4,4,4,4]
+GROUPS = [1,1,2,4,4,4,4,4,4,2,2]
 LOADS = [("x", 0, 1), ("w", 0, 1), ("w", 1, 1), ("w", 2, 1), ("w", 3, 1), ("x", 1, 1), ("x", 2, 2),
-         ("w", 4, 1), ("w", 5, 1), ("w", 6, 1), ("w", 7, 1), ("x", 4, 4), ("x", 8, 8), ("x", 16, 16)]
+         ("w", 4, 1), ("w", 5, 1), ("w", 6, 1), ("w", 7, 1), ("x", 4, 4), ("x", 8, 4), ("x", 12, 4), ("x", 16, 8), ("x", 24, 8)]
 UNITS = [8,8,8,4,4,4,4,4,4,2,2,2,2,2,2,2,1,1]
-QPOS = 2
-VIA_MOD = 4
-VIA_TAIL_FROM = 0
-VIA_TAIL_MOD = 0
 WARM = 0
 WARM_EACH = 0
 
@@ -38,20 +35,21 @@ def tile_groupfc_kernel(tc, data, W, b, out):
     assert sum(GROUPS) == NT and sum(UNITS) == 2 * NT
     with ExitStack() as ctx:
         const = ctx.enter_context(tc.tile_pool(name="const", bufs=1))
-        grp = ctx.enter_context(tc.tile_pool(name="grp", bufs=2))
+        grp = ctx.enter_context(tc.tile_pool(name="grp", bufs=3))
         stage = ctx.enter_context(tc.tile_pool(name="stage", bufs=4))
-        psum = ctx.enter_context(tc.psum_pool(name="psum", bufs=8))
+        psum = ctx.enter_context(tc.psum_pool(name="psum", bufs=1))
         ctx.enter_context(tc.manual_schedule())
 
         data_v = data.rearrange("(p t) k -> p (t k)", t=NT)
         out_v = out.rearrange("(p t) n -> p (t n)", t=NT)
         w_v = W.rearrange("(t p) k -> t p k", p=P)
 
+        b1 = const.tile([1, N], BF16, name="b1")
+        nc.scalar.dma_start(out=b1[:], in_=b.unsqueeze(0))
         ones = const.tile([P, P], BF16, name="ones")
         nc.vector.memset(ones[:], 1.0)
         brow = const.tile([P, N], BF16, name="brow")
         nc.vector.memset(brow[:], 0.0)
-        nc.scalar.dma_start(out=brow[0:1, :], in_=b.unsqueeze(0))
         scr = const.tile([P, 8], F32, name="scr")
         nc.scalar.copy(out=scr[:, 0:1], in_=ones[:, 0:1])
         ident = const.tile([P, P], F32, name="ident")
@@ -70,6 +68,7 @@ def tile_groupfc_kernel(tc, data, W, b, out):
                 nc.sync.dma_start(out=xt[:], in_=data_v[:, t0 * K:(t0 + n) * K])
                 for i in range(n):
                     x_at[t0 + i] = (xt[:].bitcast(F32), i * KW)
+        nc.vector.tensor_copy(out=brow[0:1, :], in_=b1[:])
 
         gw = []
         gw_f = []
@@ -82,41 +81,34 @@ def tile_groupfc_kernel(tc, data, W, b, out):
             wq.append(const.tile([P, 2 * NB], U32, name="wq%d" % h, align_bytes=64))
             ws.append(const.tile([P, 2 * NB], U8, name="ws%d" % h, align_bytes=64))
 
+        ring = [0]
+
+        def new_bank():
+            i = ring[0] % BANKS
+            ring[0] += 1
+            return psum.tile([P, NB], F32, name="ps%d" % i, tag="ps%d" % i)
+
         def dummies(n):
             if n > 0:
-                dm = psum.tile([P, NB], F32, name="dm", tag="ps")
+                dm = new_bank()
                 for i in range(n):
-                    nc.tensor.matmul(out=dm[:], lhsT=ones[:], rhs=brow[:, 0:NB], start=True, stop=True)
+                    nc.tensor.matmul(out=dm[:], lhsT=ones[:], rhs=brow[:, NB:2 * NB], start=True, stop=True)
 
         def transposes(src_f32, off):
-            pt = psum.tile([P, NB], F32, name="pt", tag="ps")
+            pt = new_bank()
             for c in range(4):
                 nc.tensor.transpose(pt[:, c * P:(c + 1) * P], src_f32[:, off + c * P: off + (c + 1) * P], ident[:])
             return pt[:].rearrange("p (g u r) -> p g r u", g=2, u=2)
 
-        def tw(t, eng):
+        def tw(t):
             h = t // 4
             n0 = (t % 4) * P
-            src_f32 = w_sb[t][:].bitcast(F32)
-            if eng == 2:
-                for g in range(2):
-                    ph = psum.tile([P, NB], F32, name="ph", tag="ps")
-                    for u in range(2):
-                        c = 2 * g + u
-                        nc.tensor.transpose(ph[:, u * P:(u + 1) * P], src_f32[:, c * P:(c + 1) * P], ident[:])
-                    src = ph[:, 0:2 * P].rearrange("p (u r) -> p r u", u=2)
-                    dst = gw_f[h][:, g, n0:n0 + P, :]
-                    if g == 0:
-                        nc.vector.tensor_copy(out=dst, in_=src)
-                    else:
-                        nc.scalar.copy(out=dst, in_=src)
+            src = transposes(w_sb[t][:].bitcast(F32), 0)
+            dst = gw_f[h][:, :, n0:n0 + P, :]
+            if t % 2 == 0:
+                nc.scalar.copy(out=dst, in_=src)
             else:
-                src = transposes(src_f32, 0)
-                dst = gw_f[h][:, :, n0:n0 + P, :]
-                if eng == 0:
-                    nc.scalar.copy(out=dst, in_=src)
-                else:
-                    nc.vector.tensor_copy(out=dst, in_=src)
+                nc.vector.tensor_copy(out=dst, in_=src)
             dummies(WARM_EACH)
 
         def qw(t):
@@ -168,11 +160,6 @@ def tile_groupfc_kernel(tc, data, W, b, out):
                 unit_of.append(i)
         staging = {}
 
-        def via(bk):
-            if VIA_TAIL_MOD > 0 and bk >= VIA_TAIL_FROM:
-                return bk % VIA_TAIL_MOD == 1
-            return VIA_MOD > 0 and bk % VIA_MOD == 1
-
         def bank(j, l, h):
             t = first[j] + l
             bk = 2 * t + h
@@ -180,7 +167,7 @@ def tile_groupfc_kernel(tc, data, W, b, out):
             if s not in staging:
                 staging[s] = stage.tile([P, ST * N], F32, name="ot", tag="ot")
             ot = staging[s]
-            acc = psum.tile([P, NB], F32, name="acc", tag="ps")
+            acc = new_bank()
             for g in range(2):
                 a0 = l * QT + g * P
                 nc.tensor.matmul_mx(
@@ -193,12 +180,7 @@ def tile_groupfc_kernel(tc, data, W, b, out):
                     stop=(g == 1),
                 )
             o0 = (bk % (2 * ST)) * NB
-            bs = bias[:, h * NB:(h + 1) * NB]
-            if via(bk):
-                nc.scalar.copy(out=ot[:, o0:o0 + NB], in_=acc[:])
-                nc.gpsimd.tensor_tensor(out=ot[:, o0:o0 + NB], in0=ot[:, o0:o0 + NB], in1=bs, op=ADD)
-            else:
-                nc.vector.tensor_tensor(out=ot[:, o0:o0 + NB], in0=acc[:], in1=bs, op=ADD)
+            nc.vector.tensor_tensor(out=ot[:, o0:o0 + NB], in0=acc[:], in1=bias[:, h * NB:(h + 1) * NB], op=ADD)
             i = unit_of[bk]
             left[i] -= 1
             if left[i] == 0:
@@ -207,55 +189,52 @@ def tile_groupfc_kernel(tc, data, W, b, out):
                 w = UNITS[i] * NB
                 nc.sync.dma_start(out=out_v[:, b0 * NB:b0 * NB + w], in_=ot[:, c0:c0 + w])
 
-        def mm(j, hs, nxt):
-            k = 0
-            kq = min(QPOS, len(hs) * GROUPS[j])
+        def mm(j, hs):
             for l in range(GROUPS[j]):
                 for h in hs:
                     bank(j, l, h)
-                    k += 1
-                    if nxt is not None and k == kq:
-                        qx(nxt)
 
         dummies(WARM)
         tr(0)
-        tw(0, 0)
-        tw(1, 1)
+        tw(0)
+        tw(1)
         qx(0)
         qw(0)
-        tw(2, 0)
+        tw(2)
         qw(1)
-        tw(3, 2)
+        tw(3)
         qw(2)
-        qw(3)
         tr(1)
-        tr(2)
         for h in range(2):
-            pb = psum.tile([P, NB], F32, name="pb", tag="ps")
+            pb = new_bank()
             nc.tensor.matmul(out=pb[:], lhsT=ones[:], rhs=brow[:, h * NB:(h + 1) * NB], start=True, stop=True)
             nc.scalar.copy(out=bias[:, h * NB:(h + 1) * NB], in_=pb[:])
+        qw(3)
+        tr(2)
         qx(1)
+        tw(4)
+        tw(5)
         qx(2)
-        mm(0, [0], None)
-        mm(1, [0], None)
-        mm(2, [0], None)
-        tw(4, 0)
-        tw(5, 1)
         qw(4)
-        tw(6, 0)
+        tw(6)
         qw(5)
-        tw(7, 2)
+        tw(7)
         qw(6)
         qw(7)
+        mm(0, [0])
+        mm(1, [0])
+        mm(2, [0])
         tr(3)
-        mm(0, [1], None)
-        mm(1, [1], None)
+        mm(0, [1])
+        mm(1, [1])
+        tr(4)
         qx(3)
-        mm(2, [1], None)
+        mm(2, [1])
+        qx(4)
         ng = len(GROUPS)
         for j in range(HEAD, ng):
-            if j + 1 < ng:
-                tr(j + 1)
-                mm(j, [0, 1], j + 1)
-            else:
-                mm(j, [0, 1], None)
+            if j + 2 < ng:
+                tr(j + 2)
+            mm(j, [0, 1])
+            if j + 2 < ng:
+                qx(j + 2)

from contextlib import ExitStack

import concourse.mybir as mybir
from concourse.masks import make_identity

F32 = mybir.dt.float32
BF16 = mybir.dt.bfloat16
U32 = mybir.dt.uint32
U8 = mybir.dt.uint8
FP8X4 = mybir.dt.float8_e4m3fn_x4
ADD = mybir.AluOpType.add

P = 128
B = 4096
K = 1024
N = 1024
FLOPS = 2 * B * K * N
NT = B // P
KW = K // 2
NB = 512
QT = 256
ST = 4
BANKS = 8

GROUPS = [1,1,2,4,4,4,4,4,4,2,2]
LOADS = [("x", 0, 1), ("w", 0, 1), ("w", 1, 1), ("w", 2, 1), ("w", 3, 1), ("x", 1, 1), ("x", 2, 2),
         ("w", 4, 1), ("w", 5, 1), ("w", 6, 1), ("w", 7, 1), ("x", 4, 4), ("x", 8, 4), ("x", 12, 4), ("x", 16, 8), ("x", 24, 8)]
UNITS = [8,8,8,4,4,4,4,4,4,2,2,2,2,2,2,2,1,1]
WARM = 0
WARM_EACH = 0


def tile_groupfc_kernel(tc, data, W, b, out):
    nc = tc.nc
    assert sum(GROUPS) == NT and sum(UNITS) == 2 * NT
    with ExitStack() as ctx:
        const = ctx.enter_context(tc.tile_pool(name="const", bufs=1))
        grp = ctx.enter_context(tc.tile_pool(name="grp", bufs=3))
        stage = ctx.enter_context(tc.tile_pool(name="stage", bufs=4))
        psum = ctx.enter_context(tc.psum_pool(name="psum", bufs=1))
        ctx.enter_context(tc.manual_schedule())

        data_v = data.rearrange("(p t) k -> p (t k)", t=NT)
        out_v = out.rearrange("(p t) n -> p (t n)", t=NT)
        w_v = W.rearrange("(t p) k -> t p k", p=P)

        b1 = const.tile([1, N], BF16, name="b1")
        nc.scalar.dma_start(out=b1[:], in_=b.unsqueeze(0))
        ones = const.tile([P, P], BF16, name="ones")
        nc.vector.memset(ones[:], 1.0)
        brow = const.tile([P, N], BF16, name="brow")
        nc.vector.memset(brow[:], 0.0)
        scr = const.tile([P, 8], F32, name="scr")
        nc.scalar.copy(out=scr[:, 0:1], in_=ones[:, 0:1])
        ident = const.tile([P, P], F32, name="ident")
        make_identity(nc, ident[:])
        bias = const.tile([P, N], F32, name="bias")

        w_sb = {}
        x_at = {}
        for kind, t0, n in LOADS:
            if kind == "w":
                wt = const.tile([P, K], BF16, name="w%d" % t0)
                nc.sync.dma_start(out=wt[:], in_=w_v[t0])
                w_sb[t0] = wt
            else:
                xt = const.tile([P, n * K], BF16, name="x%d" % t0)
                nc.sync.dma_start(out=xt[:], in_=data_v[:, t0 * K:(t0 + n) * K])
                for i in range(n):
                    x_at[t0 + i] = (xt[:].bitcast(F32), i * KW)
        nc.vector.tensor_copy(out=brow[0:1, :], in_=b1[:])

        gw = []
        gw_f = []
        wq = []
        ws = []
        for h in range(2):
            gwh = const.tile([P, 2 * NB * 4], BF16, name="gw%d" % h, align_bytes=64)
            gw.append(gwh)
            gw_f.append(gwh[:].bitcast(F32).rearrange("p (g n u) -> p g n u", g=2, u=2))
            wq.append(const.tile([P, 2 * NB], U32, name="wq%d" % h, align_bytes=64))
            ws.append(const.tile([P, 2 * NB], U8, name="ws%d" % h, align_bytes=64))

        ring = [0]

        def new_bank():
            i = ring[0] % BANKS
            ring[0] += 1
            return psum.tile([P, NB], F32, name="ps%d" % i, tag="ps%d" % i)

        def dummies(n):
            if n > 0:
                dm = new_bank()
                for i in range(n):
                    nc.tensor.matmul(out=dm[:], lhsT=ones[:], rhs=brow[:, NB:2 * NB], start=True, stop=True)

        def transposes(src_f32, off):
            pt = new_bank()
            for c in range(4):
                nc.tensor.transpose(pt[:, c * P:(c + 1) * P], src_f32[:, off + c * P: off + (c + 1) * P], ident[:])
            return pt[:].rearrange("p (g u r) -> p g r u", g=2, u=2)

        def tw(t):
            h = t // 4
            n0 = (t % 4) * P
            src = transposes(w_sb[t][:].bitcast(F32), 0)
            dst = gw_f[h][:, :, n0:n0 + P, :]
            if t % 2 == 0:
                nc.scalar.copy(out=dst, in_=src)
            else:
                nc.vector.tensor_copy(out=dst, in_=src)
            dummies(WARM_EACH)

        def qw(t):
            h = t // 4
            for g in range(2):
                c0 = g * NB + (t % 4) * P
                nc.vector.quantize_mx(
                    out=wq[h][:, c0:c0 + P].bitcast(FP8X4),
                    scales=ws[h][:, c0:c0 + P],
                    in_=gw[h][:, 4 * c0:4 * (c0 + P)],
                )

        xg = {}
        xq = {}
        xs = {}
        first = [sum(GROUPS[:j]) for j in range(len(GROUPS))]
        HEAD = 3

        def tr(j):
            r = GROUPS[j]
            if j < HEAD:
                xg[j] = const.tile([P, r * K], BF16, name="xgh%d" % j, align_bytes=64)
            else:
                xg[j] = grp.tile([P, r * K], BF16, name="xg", tag="xg", align_bytes=64)
            xg_f = xg[j][:].bitcast(F32)
            for l in range(r):
                src_f32, off = x_at[first[j] + l]
                src = transposes(src_f32, off)
                dst = xg_f[:, l * KW:(l + 1) * KW].rearrange("p (g r u) -> p g r u", g=2, u=2)
                nc.scalar.copy(out=dst, in_=src)

        def qx(j):
            r = GROUPS[j]
            if j < HEAD:
                xq[j] = const.tile([P, r * QT], U32, name="xqh%d" % j, align_bytes=64)
                xs[j] = const.tile([P, r * QT], U8, name="xsh%d" % j, align_bytes=64)
            else:
                xq[j] = grp.tile([P, r * QT], U32, name="xq", tag="xq", align_bytes=64)
                xs[j] = grp.tile([P, r * QT], U8, name="xs", tag="xs", align_bytes=64)
            nc.vector.quantize_mx(out=xq[j][:].bitcast(FP8X4), scales=xs[j][:], in_=xg[j][:])

        unit_of = []
        unit_b0 = []
        left = []
        for i in range(len(UNITS)):
            unit_b0.append(len(unit_of))
            left.append(UNITS[i])
            for k in range(UNITS[i]):
                unit_of.append(i)
        staging = {}

        def bank(j, l, h):
            t = first[j] + l
            bk = 2 * t + h
            s = t // ST
            if s not in staging:
                staging[s] = stage.tile([P, ST * N], F32, name="ot", tag="ot")
            ot = staging[s]
            acc = new_bank()
            for g in range(2):
                a0 = l * QT + g * P
                nc.tensor.matmul_mx(
                    out=acc[:],
                    lhsT=xq[j][:, a0:a0 + P].bitcast(FP8X4),
                    lhsT_scale=xs[j][:, a0:a0 + P],
                    rhs=wq[h][:, g * NB:(g + 1) * NB].bitcast(FP8X4),
                    rhs_scale=ws[h][:, g * NB:(g + 1) * NB],
                    start=(g == 0),
                    stop=(g == 1),
                )
            o0 = (bk % (2 * ST)) * NB
            nc.vector.tensor_tensor(out=ot[:, o0:o0 + NB], in0=acc[:], in1=bias[:, h * NB:(h + 1) * NB], op=ADD)
            i = unit_of[bk]
            left[i] -= 1
            if left[i] == 0:
                b0 = unit_b0[i]
                c0 = (b0 % (2 * ST)) * NB
                w = UNITS[i] * NB
                nc.sync.dma_start(out=out_v[:, b0 * NB:b0 * NB + w], in_=ot[:, c0:c0 + w])

        def mm(j, hs):
            for l in range(GROUPS[j]):
                for h in hs:
                    bank(j, l, h)

        dummies(WARM)
        tr(0)
        tw(0)
        tw(1)
        qx(0)
        qw(0)
        tw(2)
        qw(1)
        tw(3)
        qw(2)
        tr(1)
        for h in range(2):
            pb = new_bank()
            nc.tensor.matmul(out=pb[:], lhsT=ones[:], rhs=brow[:, h * NB:(h + 1) * NB], start=True, stop=True)
            nc.scalar.copy(out=bias[:, h * NB:(h + 1) * NB], in_=pb[:])
        qw(3)
        tr(2)
        qx(1)
        tw(4)
        tw(5)
        qx(2)
        qw(4)
        tw(6)
        qw(5)
        tw(7)
        qw(6)
        qw(7)
        mm(0, [0])
        mm(1, [0])
        mm(2, [0])
        tr(3)
        mm(0, [1])
        mm(1, [1])
        tr(4)
        qx(3)
        mm(2, [1])
        qx(4)
        ng = len(GROUPS)
        for j in range(HEAD, ng):
            if j + 2 < ng:
                tr(j + 2)
            mm(j, [0, 1])
            if j + 2 < ng:
                qx(j + 2)
